import numpy as np
import ml_dtypes


def mxq(x, axis, fmt="e4m3"):
    dtype, down = {"e4m3": (ml_dtypes.float8_e4m3fn, 7), "e5m2": (ml_dtypes.float8_e5m2, 14)}[fmt]
    v = np.moveaxis(np.asarray(x, np.float32).astype(ml_dtypes.bfloat16).astype(np.float64), axis, -1)
    blocks = v.reshape(v.shape[:-1] + (-1, 32))
    amax = np.abs(blocks).max(-1, keepdims=True)
    byte = np.maximum(np.where(amax > 0, np.frexp(amax)[1] - 1 + 127, 0) - down, 1)
    scale = np.exp2(byte - 127.0)
    codes = (blocks / scale).astype(np.float32).astype(dtype).astype(np.float64)
    return np.moveaxis((codes * scale).reshape(v.shape), -1, axis)


WIDE = False


def mx_kscale(k):
    if not WIDE:
        return np.ones(k)
    levels = np.array([10, -10, 5, -5, 0])
    if k % 512:
        return np.exp2(np.random.permutation(np.resize(levels, k // 32))).repeat(32)
    a = np.empty((k // 512, 16))
    for p in range(k // 512):
        a[p, :8] = np.random.permutation(np.resize(levels, 8))
        for g in range(8):
            far = levels[np.abs(levels - a[p, g]) >= 10]
            a[p, g + 8] = far[np.random.randint(len(far))]
    return np.exp2(a.ravel()).repeat(32)


BF16 = ml_dtypes.bfloat16


def bf(x):
    return np.asarray(x, np.float32).astype(BF16)


def f64(x):
    return np.asarray(x).astype(np.float64)


B, S, H, HD = 8, 512, 512, 128
NH = H // HD
HALF = HD // 2
WS = 1.5 * (HD / H) ** 0.25 / np.sqrt(H)


def rotate_half(u):
    return np.concatenate((-u[..., HALF:], u[..., :HALF]), axis=-1)


def rope(u, c, s):
    u4 = u.reshape(B, S, NH, HD)
    return (u4 * c[None, :, None, :] + rotate_half(u4) * s[None, :, None, :]).reshape(B, S, H)


def draw0():
    s = mx_kscale(H)
    t = np.tile(mx_kscale(H).reshape(NH, 2, HALF)[:, :1, :], (1, 2, 1)).reshape(H)
    return {"hidden_states": bf(np.random.standard_normal((B, S, H)) * s),
            "wq_deq": bf(np.random.standard_normal((H, H)) * WS * t[:, None] / s[None, :]),
            "wk_deq": bf(np.random.standard_normal((H, H)) * WS / t[:, None] / s[None, :]),
            "cos": bf(np.random.random((S, HD))),
            "sin": bf(np.random.random((S, HD))),
            "attention_mask": bf(np.random.standard_normal((1, S, S)) * 0.5)}


def core(hidden_states, wq_deq, wk_deq, cos, sin, attention_mask):
    xq = mxq(f64(hidden_states), 2, "e4m3")
    q = xq @ mxq(f64(wq_deq), 1, "e4m3").T
    k = xq @ mxq(f64(wk_deq), 1, "e4m3").T
    q_rot = rope(q, f64(cos), f64(sin))
    k_rot = rope(k, f64(cos), f64(sin))
    scores = (mxq(q_rot, 2, "e4m3") @ mxq(k_rot, 2, "e4m3").transpose(0, 2, 1)) / np.sqrt(HD)
    return scores + f64(attention_mask)


def e4m3fn_bytes(y):
    return np.clip(np.asarray(y, np.float64), -448.0, 448.0).astype(np.float32).astype(ml_dtypes.float8_e4m3fn).view(np.uint8)


def e4m3fn_values(b):
    return np.asarray(b, np.uint8).view(ml_dtypes.float8_e4m3fn).astype(np.float64)


def setup_inputs():
    d = draw0()
    x0 = np.asarray(d['hidden_states']).astype(np.float64)
    s = (np.max(np.abs(x0), axis=(0, 1), keepdims=True) / 448.0).astype(np.float32)
    out = {}
    for k, v in d.items():
        if k == 'hidden_states':
            out['hidden_states_bytes'] = e4m3fn_bytes(x0 / s.astype(np.float64))
            out['hidden_states_scale'] = s
        else:
            out[k] = v
    return out


def reference(hidden_states_bytes, hidden_states_scale, wq_deq, wk_deq, cos, sin, attention_mask):
    return core(e4m3fn_values(hidden_states_bytes) * hidden_states_scale.astype(np.float64), wq_deq, wk_deq, cos, sin, attention_mask)

@@ -1,0 +1,325 @@
+from contextlib import ExitStack
+
+import concourse.mybir as mybir
+from concourse.masks import make_identity
+
+F32 = mybir.dt.float32
+BF16 = mybir.dt.bfloat16
+U32 = mybir.dt.uint32
+U8 = mybir.dt.uint8
+FP8 = mybir.dt.float8_e4m3fn
+FP8X4 = mybir.dt.float8_e4m3fn_x4
+MULT = mybir.AluOpType.mult
+ADD = mybir.AluOpType.add
+
+B, S, H, HD = 8, 512, 512, 128
+P = 128
+TILES = S // P
+N_TILES = B * TILES
+FLOPS = 2 * B * S * H * H * 2 + 2 * B * S * S * H
+SCORE_SCALE = 1.0 / HD**0.5
+SCORE_LAG = 6
+
+
+def tile_llamaattention_pa_t_kernel(tc, x_bytes, x_scale, wq, wk, cos, sin, mask, out):
+    nc = tc.nc
+    with ExitStack() as ctx:
+        keep = ctx.enter_context(tc.tile_pool(name="keep", bufs=1))
+        work = ctx.enter_context(tc.tile_pool(name="work", bufs=3))
+        psum = ctx.enter_context(tc.psum_pool(name="psum", bufs=1))
+
+        def bank(tag, bufs):
+            t = psum.tile([P, 512], F32, name=tag, tag=tag, bufs=bufs)
+            return t
+
+        scale_sb = keep.tile([P, 1, 4], F32, name="scale_sb")
+        wq_sb = keep.tile([P, 4, H], BF16, name="wq_sb")
+        wk_sb = keep.tile([P, 4, H], BF16, name="wk_sb")
+        cos_sb = keep.tile([P, TILES, HD], BF16, name="cos_sb")
+        sin_sb = keep.tile([P, TILES, HD], BF16, name="sin_sb")
+        mask_sb = keep.tile([P, TILES, S], BF16, name="mask_sb")
+        x_sb = []
+        for b in range(B):
+            xb = keep.tile([P, TILES * H], U8, name="x_bytes_sb%d" % b)
+            x_sb.append(xb)
+
+        def load_x(b, h0, h1):
+            src = x_bytes[b].rearrange("(p j) k -> p (j k)", j=TILES)
+            nc.sync.dma_start(out=x_sb[b][:, h0:h1], in_=src[:, h0:h1])
+
+        load_x(0, 0, 1024)
+        nc.scalar.dma_start(out=scale_sb[:], in_=x_scale.rearrange("a b (p t) -> p (a b) t", t=4))
+        nc.sync.dma_start(out=wq_sb[:], in_=wq.rearrange("(p t) k -> p t k", t=4))
+        nc.sync.dma_start(out=wk_sb[:], in_=wk.rearrange("(p t) k -> p t k", t=4))
+        nc.scalar.dma_start(out=cos_sb[:], in_=cos.rearrange("(p j) d -> p j d", j=TILES))
+        nc.scalar.dma_start(out=sin_sb[:], in_=sin.rearrange("(p j) d -> p j d", j=TILES))
+        load_x(0, 1024, 2048)
+        load_x(1, 0, 2048)
+        nc.sync.dma_start(out=mask_sb[:], in_=mask.rearrange("a (p j) n -> p (a j) n", j=TILES))
+        for b in range(2, B):
+            load_x(b, 0, 2048)
+
+        ident = keep.tile([P, P], F32, name="ident")
+        make_identity(nc, ident[:])
+
+        cos_t = keep.tile([P, TILES, 4, 4, 32], BF16, name="cos_t")
+        sin_t = keep.tile([P, TILES, 4, 4, 2, 16], BF16, name="sin_t")
+
+        w_codes = {}
+        w_scales = {}
+        for w in ("q", "k"):
+            wc = keep.tile([P, H], U32, name="w_codes_" + w, align_bytes=64)
+            ws = keep.tile([P, H], U8, name="w_scales_" + w, align_bytes=64)
+            w_codes[w] = wc
+            w_scales[w] = ws
+
+        x_wide = {}
+        x_t = {}
+        x_grouped = {}
+        x_codes = {}
+        x_scales = {}
+        q_ps = {}
+        k_ps = {}
+        k_sb = {}
+        prod = {}
+        rot_ps = {}
+        rot_grouped = {}
+        rot_codes = {}
+        rot_scales = {}
+        score_ps = {}
+        out_sb = {}
+
+        def widen(m):
+            xw = work.tile([P, 2 * H], BF16, name="x_wide", bufs=2)
+            half = x_sb[m // 2][:, (m % 2) * 1024 : (m % 2) * 1024 + 1024]
+            nc.scalar.copy(out=xw[:], in_=half.bitcast(FP8))
+            x_wide[m] = xw
+
+        def transpose_x(m):
+            xt = bank("xt", 1)
+            words = x_wide[m][:].bitcast(F32)
+            for j in range(2):
+                for u in range(2):
+                    nc.tensor.transpose(
+                        xt[:, u * 256 + j * P : u * 256 + (j + 1) * P],
+                        words[:, 256 * j + u : 256 * (j + 1) : 2],
+                        ident[:],
+                    )
+            x_t[m] = xt
+
+        def scale_x(m):
+            xg = work.tile([P, 256, 4], BF16, name="x_grouped", bufs=2, align_bytes=64)
+            nc.vector.tensor_tensor(
+                out=xg[:].rearrange("p r (u e) -> p r u e", e=2),
+                in0=x_t[m][:].bitcast(BF16).rearrange("p (u r e) -> p r u e", u=2, e=2),
+                in1=scale_sb[:].to_broadcast([P, 256, 4]).rearrange("p r (u e) -> p r u e", e=2),
+                op=MULT,
+            )
+            x_grouped[m] = xg
+
+        def quantize_x(m):
+            xc = work.tile([P, 256], U32, name="x_codes", align_bytes=64)
+            xs = work.tile([P, 256], U8, name="x_scales", align_bytes=64)
+            nc.vector.quantize_mx(
+                out=xc[:].bitcast(FP8X4), scales=xs[:], in_=x_grouped[m][:].rearrange("p r t -> p (r t)")
+            )
+            x_codes[m] = xc
+            x_scales[m] = xs
+
+        def project(i):
+            m, j = divmod(i, 2)
+            cols = slice(j * P, (j + 1) * P)
+            for w, ps, bufs in (("k", k_ps, 1), ("q", q_ps, 2)):
+                acc = bank(w + "_ps", bufs)
+                nc.tensor.matmul_mx(
+                    out=acc[:],
+                    lhsT=x_codes[m][:, cols].bitcast(FP8X4),
+                    lhsT_scale=x_scales[m][:, cols],
+                    rhs=w_codes[w][:].bitcast(FP8X4),
+                    rhs_scale=w_scales[w][:],
+                    start=True,
+                    stop=True,
+                )
+                ps[i] = acc
+
+        def copy_k(i):
+            kf = work.tile([P, H], F32, name="k_sb", bufs=2)
+            nc.scalar.copy(out=kf[:], in_=k_ps[i][:])
+            k_sb[i] = kf
+
+        def rope_products(engine, w, i, src):
+            jj = i % TILES
+            direct = work.tile([P, H], F32, name="direct_" + w, bufs=2)
+            engine.tensor_tensor(
+                out=direct[:], in0=src[:], in1=cos_t[:, jj].rearrange("p t u d -> p (t u d)"), op=MULT
+            )
+            crossed = work.tile([P, H], F32, name="crossed_" + w, bufs=2)
+            engine.tensor_tensor(
+                out=crossed[:].rearrange("p (a h c) -> p a h c", h=2, c=16),
+                in0=src[:].rearrange("p (a h c) -> p a h c", h=2, c=16)[:, :, ::-1, :],
+                in1=sin_t[:, jj].rearrange("p t u h c -> p (t u) h c"),
+                op=MULT,
+            )
+            prod[w, i] = (direct, crossed)
+
+        def sum_and_turn(w, i):
+            rot = bank("rot", 2)
+            direct, crossed = prod[w, i]
+            for t in range(4):
+                cols = slice(t * P, (t + 1) * P)
+                nc.tensor.matmul(
+                    rot[:, cols], lhsT=direct[:, cols], rhs=ident[:], start=True, stop=False, is_transpose=True
+                )
+                nc.tensor.matmul(
+                    rot[:, cols], lhsT=crossed[:, cols], rhs=ident[:], start=False, stop=True, is_transpose=True
+                )
+            rot_ps[w, i] = rot
+
+        def round_rot(w, i):
+            m, j = divmod(i, 2)
+            if j == 0:
+                rg = work.tile([P, 256, 4], BF16, name="rot_grouped_" + w, bufs=2, align_bytes=64)
+                rot_grouped[w, m] = rg
+            nc.scalar.copy(
+                out=rot_grouped[w, m][:, j * P : (j + 1) * P, :],
+                in_=rot_ps[w, i][:].rearrange("p (t r) -> p r t", t=4),
+            )
+
+        def quantize_rot(w, m):
+            b, h = divmod(m, 2)
+            if h == 0:
+                rc = work.tile([P, S], U32, name="rot_codes_" + w, align_bytes=64)
+                rs = work.tile([P, S], U8, name="rot_scales_" + w, align_bytes=64)
+                rot_codes[w, b] = rc
+                rot_scales[w, b] = rs
+            cols = slice(h * 256, (h + 1) * 256)
+            nc.vector.quantize_mx(
+                out=rot_codes[w, b][:, cols].bitcast(FP8X4),
+                scales=rot_scales[w, b][:, cols],
+                in_=rot_grouped[w, m][:].rearrange("p r t -> p (r t)"),
+            )
+
+        def score(n):
+            b, jj = divmod(n, TILES)
+            cols = slice(jj * P, (jj + 1) * P)
+            acc = bank("score", 2)
+            nc.tensor.matmul_mx(
+                out=acc[:],
+                lhsT=rot_codes["q", b][:, cols].bitcast(FP8X4),
+                lhsT_scale=rot_scales["q", b][:, cols],
+                rhs=rot_codes["k", b][:].bitcast(FP8X4),
+                rhs_scale=rot_scales["k", b][:],
+                start=True,
+                stop=True,
+            )
+            score_ps[n] = acc
+
+        def finish(n):
+            b, jj = divmod(n, TILES)
+            if jj % 2 == 0:
+                o = work.tile([P, 2, S], F32, name="out_sb")
+                out_sb[n // 2] = o
+            o = out_sb[n // 2]
+            nc.vector.scalar_tensor_tensor(
+                out=o[:, jj % 2, :].rearrange("p (r j) -> p r j", j=TILES),
+                in0=score_ps[n][:].rearrange("p (j r) -> p r j", j=TILES),
+                scalar=SCORE_SCALE,
+                in1=mask_sb[:, jj, :].rearrange("p (r j) -> p r j", j=TILES),
+                op0=MULT,
+                op1=ADD,
+            )
+            if jj % 2 == 1:
+                rows = out[b].rearrange("(p j) n -> p j n", j=TILES)
+                nc.sync.dma_start(out=rows[:, jj - 1 : jj + 1, :], in_=o[:])
+
+        def prepare_w(w, w_sb):
+            wg = keep.tile([P, H, 4], BF16, name="w_grouped_" + w, align_bytes=64)
+            words = w_sb[:].rearrange("p t k -> p (t k)").bitcast(F32)
+            for g in range(2):
+                wt = bank("rot", 2)
+                for jt in range(2):
+                    t = 2 * g + jt
+                    for u in range(2):
+                        nc.tensor.transpose(
+                            wt[:, u * 256 + jt * P : u * 256 + (jt + 1) * P],
+                            words[:, 256 * t + u : 256 * (t + 1) : 2],
+                            ident[:],
+                        )
+                copy = nc.vector.tensor_copy if g == 0 else nc.scalar.copy
+                copy(
+                    out=wg[:, g * 256 : (g + 1) * 256, :].rearrange("p f t -> p (f t)").bitcast(F32),
+                    in_=wt[:].rearrange("p (u f) -> p f u", u=2),
+                )
+            nc.vector.quantize_mx(
+                out=w_codes[w][:].bitcast(FP8X4), scales=w_scales[w][:], in_=wg[:].rearrange("p f t -> p (f t)")
+            )
+
+        def build_tables():
+            for u in range(4):
+                nc.gpsimd.tensor_scalar(
+                    out=cos_t[:, :, :, u, :],
+                    in0=cos_sb[:].rearrange("p j (d t) -> p j t d", t=4),
+                    scalar1=1.0,
+                    scalar2=0.0,
+                    op0=MULT,
+                    op1=ADD,
+                )
+            for u in range(4):
+                for h in range(2):
+                    nc.gpsimd.tensor_scalar(
+                        out=sin_t[:, :, :, u, h, :],
+                        in0=sin_sb[:].rearrange("p j (h d t) -> p j t h d", h=2, t=4)[:, :, :, h, :],
+                        scalar1=-1.0 if h == 0 else 1.0,
+                        scalar2=0.0,
+                        op0=MULT,
+                        op1=ADD,
+                    )
+
+        n_pairs = N_TILES // 2
+
+        def slot(i):
+            if 0 <= i + 1 < N_TILES:
+                project(i + 1)
+            n = i - SCORE_LAG
+            if 0 <= n < N_TILES:
+                score(n)
+            if 0 <= i - 1 < N_TILES:
+                round_rot("q", i - 1)
+            if 0 <= i + 1 < N_TILES:
+                copy_k(i + 1)
+            if 0 <= i < N_TILES:
+                rope_products(nc.vector, "q", i, q_ps[i])
+                rope_products(nc.gpsimd, "k", i, k_sb[i])
+            m, odd = divmod(i, 2)
+            if odd and m + 2 < n_pairs:
+                transpose_x(m + 2)
+            if 0 <= i - 1 < N_TILES:
+                sum_and_turn("k", i - 1)
+            if 0 <= i < N_TILES:
+                sum_and_turn("q", i)
+            if 0 <= i - 1 < N_TILES:
+                round_rot("k", i - 1)
+            if not odd and 0 <= m + 2 < n_pairs:
+                widen(m + 2)
+            if odd:
+                if m + 2 < n_pairs:
+                    scale_x(m + 2)
+                if 0 <= m - 1 < n_pairs:
+                    quantize_rot("k", m - 1)
+            else:
+                if 0 <= m - 1 < n_pairs:
+                    quantize_rot("q", m - 1)
+                if 0 <= m + 1 < n_pairs:
+                    quantize_x(m + 1)
+            if 0 <= n < N_TILES:
+                finish(n)
+
+        with tc.manual_schedule():
+            build_tables()
+            slot(-4)
+            prepare_w("q", wq_sb)
+            slot(-3)
+            slot(-2)
+            prepare_w("k", wk_sb)
+            for i in range(-1, N_TILES + SCORE_LAG):
+                slot(i)

@@ -18,7 +18,7 @@ TILES = S // P
 N_TILES = B * TILES
 FLOPS = 2 * B * S * H * H * 2 + 2 * B * S * S * H
 SCORE_SCALE = 1.0 / HD**0.5
-SCORE_LAG = 6
+WHICH = {"q": 0, "k": 1}
 
 
 def tile_llamaattention_pa_t_kernel(tc, x_bytes, x_scale, wq, wk, cos, sin, mask, out):
@@ -48,22 +48,27 @@ def tile_llamaattention_pa_t_kernel(tc, x_bytes, x_scale, wq, wk, cos, sin, mask
             nc.sync.dma_start(out=x_sb[b][:, h0:h1], in_=src[:, h0:h1])
 
         load_x(0, 0, 1024)
-        nc.scalar.dma_start(out=scale_sb[:], in_=x_scale.rearrange("a b (p t) -> p (a b) t", t=4))
-        nc.sync.dma_start(out=wq_sb[:], in_=wq.rearrange("(p t) k -> p t k", t=4))
-        nc.sync.dma_start(out=wk_sb[:], in_=wk.rearrange("(p t) k -> p t k", t=4))
         nc.scalar.dma_start(out=cos_sb[:], in_=cos.rearrange("(p j) d -> p j d", j=TILES))
         nc.scalar.dma_start(out=sin_sb[:], in_=sin.rearrange("(p j) d -> p j d", j=TILES))
+        nc.scalar.dma_start(out=scale_sb[:], in_=x_scale.rearrange("a b (p t) -> p (a b) t", t=4))
+        for w_dram, w_sb in ((wk, wk_sb), (wq, wq_sb)):
+            rows = w_dram.rearrange("(u g q t) k -> g u q t k", u=4, g=2, t=4)
+            for g in range(2):
+                for u in range(4):
+                    p0 = 64 * g + 16 * u
+                    nc.sync.dma_start(out=w_sb[p0 : p0 + 16], in_=rows[g, u])
         load_x(0, 1024, 2048)
         load_x(1, 0, 2048)
+        load_x(2, 0, 2048)
         nc.sync.dma_start(out=mask_sb[:], in_=mask.rearrange("a (p j) n -> p (a j) n", j=TILES))
-        for b in range(2, B):
+        for b in range(3, B):
             load_x(b, 0, 2048)
 
         ident = keep.tile([P, P], F32, name="ident")
         make_identity(nc, ident[:])
 
-        cos_t = keep.tile([P, TILES, 4, 4, 32], BF16, name="cos_t")
-        sin_t = keep.tile([P, TILES, 4, 4, 2, 16], BF16, name="sin_t")
+        cos_t = keep.tile([P, TILES, 4, 2, 4, 16], BF16, name="cos_t")
+        sin_t = keep.tile([P, TILES, 4, 2, 4, 16], BF16, name="sin_t")
 
         w_codes = {}
         w_scales = {}
@@ -90,7 +95,7 @@ def tile_llamaattention_pa_t_kernel(tc, x_bytes, x_scale, wq, wk, cos, sin, mask
         out_sb = {}
 
         def widen(m):
-            xw = work.tile([P, 2 * H], BF16, name="x_wide", bufs=2)
+            xw = work.tile([P, 2 * H], BF16, name="x_wide", bufs=4)
             half = x_sb[m // 2][:, (m % 2) * 1024 : (m % 2) * 1024 + 1024]
             nc.scalar.copy(out=xw[:], in_=half.bitcast(FP8))
             x_wide[m] = xw
@@ -108,7 +113,7 @@ def tile_llamaattention_pa_t_kernel(tc, x_bytes, x_scale, wq, wk, cos, sin, mask
             x_t[m] = xt
 
         def scale_x(m):
-            xg = work.tile([P, 256, 4], BF16, name="x_grouped", bufs=2, align_bytes=64)
+            xg = work.tile([P, 256, 4], BF16, name="x_grouped", bufs=4, align_bytes=64)
             nc.vector.tensor_tensor(
                 out=xg[:].rearrange("p r (u e) -> p r u e", e=2),
                 in0=x_t[m][:].bitcast(BF16).rearrange("p (u r e) -> p r u e", u=2, e=2),
@@ -118,49 +123,70 @@ def tile_llamaattention_pa_t_kernel(tc, x_bytes, x_scale, wq, wk, cos, sin, mask
             x_grouped[m] = xg
 
         def quantize_x(m):
-            xc = work.tile([P, 256], U32, name="x_codes", align_bytes=64)
-            xs = work.tile([P, 256], U8, name="x_scales", align_bytes=64)
+            xc = work.tile([P, 256], U32, name="x_codes", bufs=6, align_bytes=64)
+            xs = work.tile([P, 256], U8, name="x_scales", bufs=6, align_bytes=64)
             nc.vector.quantize_mx(
                 out=xc[:].bitcast(FP8X4), scales=xs[:], in_=x_grouped[m][:].rearrange("p r t -> p (r t)")
             )
             x_codes[m] = xc
             x_scales[m] = xs
 
-        def project(i):
+        def project(w, i):
             m, j = divmod(i, 2)
             cols = slice(j * P, (j + 1) * P)
-            for w, ps, bufs in (("k", k_ps, 1), ("q", q_ps, 2)):
-                acc = bank(w + "_ps", bufs)
-                nc.tensor.matmul_mx(
-                    out=acc[:],
-                    lhsT=x_codes[m][:, cols].bitcast(FP8X4),
-                    lhsT_scale=x_scales[m][:, cols],
-                    rhs=w_codes[w][:].bitcast(FP8X4),
-                    rhs_scale=w_scales[w][:],
-                    start=True,
-                    stop=True,
-                )
-                ps[i] = acc
+            if w == "q":
+                acc = bank("q_ps", 2)
+                q_ps[i] = acc
+            elif on_gpsimd(i):
+                acc = bank("kg_ps", 1)
+                k_ps[i] = acc
+            else:
+                acc = bank("kv_ps", 1)
+                k_ps[i] = acc
+            nc.tensor.matmul_mx(
+                out=acc[:],
+                lhsT=x_codes[m][:, cols].bitcast(FP8X4),
+                lhsT_scale=x_scales[m][:, cols],
+                rhs=w_codes[w][:].bitcast(FP8X4),
+                rhs_scale=w_scales[w][:],
+                start=True,
+                stop=True,
+            )
+
+        def on_gpsimd(i):
+            return i % 4 != 1
 
         def copy_k(i):
+            if not on_gpsimd(i):
+                return
             kf = work.tile([P, H], F32, name="k_sb", bufs=2)
             nc.scalar.copy(out=kf[:], in_=k_ps[i][:])
             k_sb[i] = kf
 
         def rope_products(engine, w, i, src):
             jj = i % TILES
-            direct = work.tile([P, H], F32, name="direct_" + w, bufs=2)
+            direct = work.tile([P, H], F32, name="direct_" + w + ("g" if engine is nc.gpsimd else "v"), bufs=2)
             engine.tensor_tensor(
-                out=direct[:], in0=src[:], in1=cos_t[:, jj].rearrange("p t u d -> p (t u d)"), op=MULT
+                out=direct[:], in0=src[:], in1=cos_t[:, jj].rearrange("p t g u q -> p (t g u q)"), op=MULT
             )
-            crossed = work.tile([P, H], F32, name="crossed_" + w, bufs=2)
+            crossed = work.tile([P, H], F32, name="crossed_" + w + ("g" if engine is nc.gpsimd else "v"), bufs=2)
             engine.tensor_tensor(
-                out=crossed[:].rearrange("p (a h c) -> p a h c", h=2, c=16),
-                in0=src[:].rearrange("p (a h c) -> p a h c", h=2, c=16)[:, :, ::-1, :],
-                in1=sin_t[:, jj].rearrange("p t u h c -> p (t u) h c"),
+                out=crossed[:].rearrange("p (t g c) -> p t g c", t=4, g=2),
+                in0=src[:].rearrange("p (t g c) -> p t g c", t=4, g=2)[:, :, ::-1, :],
+                in1=sin_t[:, jj].rearrange("p t g u q -> p t g (u q)"),
                 op=MULT,
             )
             prod[w, i] = (direct, crossed)
+
+        def products_gpsimd(i):
+            if on_gpsimd(i):
+                rope_products(nc.gpsimd, "k", i, k_sb[i])
+
+        def products_vector(w, i):
+            if w == "q":
+                rope_products(nc.vector, "q", i, q_ps[i])
+            elif not on_gpsimd(i):
+                rope_products(nc.vector, "k", i, k_ps[i])
 
         def sum_and_turn(w, i):
             rot = bank("rot", 2)
@@ -177,41 +203,40 @@ def tile_llamaattention_pa_t_kernel(tc, x_bytes, x_scale, wq, wk, cos, sin, mask
 
         def round_rot(w, i):
             m, j = divmod(i, 2)
-            if j == 0:
-                rg = work.tile([P, 256, 4], BF16, name="rot_grouped_" + w, bufs=2, align_bytes=64)
-                rot_grouped[w, m] = rg
+            if m not in rot_grouped:
+                rg = work.tile([P, 2, 256, 4], BF16, name="rot_grouped", bufs=3, align_bytes=64)
+                rot_grouped[m] = rg
             nc.scalar.copy(
-                out=rot_grouped[w, m][:, j * P : (j + 1) * P, :],
+                out=rot_grouped[m][:, WHICH[w], j * P : (j + 1) * P, :],
                 in_=rot_ps[w, i][:].rearrange("p (t r) -> p r t", t=4),
             )
 
-        def quantize_rot(w, m):
-            b, h = divmod(m, 2)
-            if h == 0:
-                rc = work.tile([P, S], U32, name="rot_codes_" + w, align_bytes=64)
-                rs = work.tile([P, S], U8, name="rot_scales_" + w, align_bytes=64)
-                rot_codes[w, b] = rc
-                rot_scales[w, b] = rs
-            cols = slice(h * 256, (h + 1) * 256)
+        def quantize_rot(m):
+            rc = work.tile([P, 2, 256], U32, name="rot_codes", bufs=5, align_bytes=64)
+            rs = work.tile([P, 2, 256], U8, name="rot_scales", bufs=5, align_bytes=64)
             nc.vector.quantize_mx(
-                out=rot_codes[w, b][:, cols].bitcast(FP8X4),
-                scales=rot_scales[w, b][:, cols],
-                in_=rot_grouped[w, m][:].rearrange("p r t -> p (r t)"),
+                out=rc[:].rearrange("p w r -> p (w r)").bitcast(FP8X4),
+                scales=rs[:].rearrange("p w r -> p (w r)"),
+                in_=rot_grouped[m][:].rearrange("p w r t -> p (w r t)"),
             )
+            rot_codes[m] = rc
+            rot_scales[m] = rs
 
         def score(n):
-            b, jj = divmod(n, TILES)
-            cols = slice(jj * P, (jj + 1) * P)
-            acc = bank("score", 2)
-            nc.tensor.matmul_mx(
-                out=acc[:],
-                lhsT=rot_codes["q", b][:, cols].bitcast(FP8X4),
-                lhsT_scale=rot_scales["q", b][:, cols],
-                rhs=rot_codes["k", b][:].bitcast(FP8X4),
-                rhs_scale=rot_scales["k", b][:],
-                start=True,
-                stop=True,
-            )
+            m, j = divmod(n, 2)
+            cols = slice(j * P, (j + 1) * P)
+            first = m - m % 2
+            acc = bank("score", 1)
+            for h in range(2):
+                nc.tensor.matmul_mx(
+                    out=acc[:, h * 256 : (h + 1) * 256],
+                    lhsT=rot_codes[m][:, 0, cols].bitcast(FP8X4),
+                    lhsT_scale=rot_scales[m][:, 0, cols],
+                    rhs=rot_codes[first + h][:, 1, :].bitcast(FP8X4),
+                    rhs_scale=rot_scales[first + h][:, 1, :],
+                    start=True,
+                    stop=True,
+                )
             score_ps[n] = acc
 
         def finish(n):
@@ -255,71 +280,72 @@ def tile_llamaattention_pa_t_kernel(tc, x_bytes, x_scale, wq, wk, cos, sin, mask
             )
 
         def build_tables():
-            for u in range(4):
-                nc.gpsimd.tensor_scalar(
-                    out=cos_t[:, :, :, u, :],
-                    in0=cos_sb[:].rearrange("p j (d t) -> p j t d", t=4),
-                    scalar1=1.0,
-                    scalar2=0.0,
-                    op0=MULT,
-                    op1=ADD,
-                )
-            for u in range(4):
-                for h in range(2):
-                    nc.gpsimd.tensor_scalar(
-                        out=sin_t[:, :, :, u, h, :],
-                        in0=sin_sb[:].rearrange("p j (h d t) -> p j t h d", h=2, t=4)[:, :, :, h, :],
-                        scalar1=-1.0 if h == 0 else 1.0,
-                        scalar2=0.0,
-                        op0=MULT,
-                        op1=ADD,
+            for g in range(2):
+                for u in range(4):
+                    nc.vector.tensor_copy(
+                        out=cos_t[:, :, :, g, u, :],
+                        in_=cos_sb[:].rearrange("p j (g q t) -> p j t g q", g=2, t=4)[:, :, :, g, :],
+                    )
+                    nc.scalar.activation(
+                        out=sin_t[:, :, :, g, u, :],
+                        in_=sin_sb[:].rearrange("p j (g q t) -> p j t g q", g=2, t=4)[:, :, :, g, :],
+                        func=mybir.ActivationFunctionType.Copy,
+                        scale=-1.0 if g == 0 else 1.0,
                     )
 
         n_pairs = N_TILES // 2
 
-        def slot(i):
-            if 0 <= i + 1 < N_TILES:
-                project(i + 1)
-            n = i - SCORE_LAG
-            if 0 <= n < N_TILES:
-                score(n)
-            if 0 <= i - 1 < N_TILES:
-                round_rot("q", i - 1)
-            if 0 <= i + 1 < N_TILES:
-                copy_k(i + 1)
-            if 0 <= i < N_TILES:
-                rope_products(nc.vector, "q", i, q_ps[i])
-                rope_products(nc.gpsimd, "k", i, k_sb[i])
-            m, odd = divmod(i, 2)
-            if odd and m + 2 < n_pairs:
-                transpose_x(m + 2)
-            if 0 <= i - 1 < N_TILES:
-                sum_and_turn("k", i - 1)
-            if 0 <= i < N_TILES:
-                sum_and_turn("q", i)
-            if 0 <= i - 1 < N_TILES:
-                round_rot("k", i - 1)
-            if not odd and 0 <= m + 2 < n_pairs:
-                widen(m + 2)
-            if odd:
-                if m + 2 < n_pairs:
-                    scale_x(m + 2)
-                if 0 <= m - 1 < n_pairs:
-                    quantize_rot("k", m - 1)
-            else:
-                if 0 <= m - 1 < n_pairs:
-                    quantize_rot("q", m - 1)
-                if 0 <= m + 1 < n_pairs:
-                    quantize_x(m + 1)
-            if 0 <= n < N_TILES:
-                finish(n)
+        order = [
+            (products_gpsimd, None, 0, -1),
+            (sum_and_turn, "k", 1, 0),
+            (products_vector, "q", 0, -1),
+            (copy_k, None, 0, -2),
+            (sum_and_turn, "k", 0, -1),
+            (products_vector, "q", 1, -1),
+            (score, None, 1, 2),
+            (round_rot, "k", 1, 0),
+            (transpose_x, None, None, -5),
+            (finish, None, 1, 2),
+            (project, "k", 1, -2),
+            (sum_and_turn, "q", 0, -1),
+            (round_rot, "k", 0, -1),
+            (quantize_x, None, None, -4),
+            (quantize_rot, None, None, 0),
+            (sum_and_turn, "q", 1, -1),
+            (products_gpsimd, None, 1, -1),
+            (products_vector, "k", 1, -1),
+            (widen, None, None, -8),
+            (scale_x, None, None, -5),
+            (round_rot, "q", 0, -1),
+            (products_vector, "k", 0, -1),
+            (project, "q", 0, -2),
+            (copy_k, None, 1, -2),
+            (score, None, 0, 1),
+            (round_rot, "q", 1, -1),
+            (project, "k", 0, -3),
+            (finish, None, 0, 1),
+            (project, "q", 1, -2),
+        ]
 
+        leads = [lead for stage, w, j, lead in order]
         with tc.manual_schedule():
+            widen(0)
+            transpose_x(0)
             build_tables()
-            slot(-4)
-            prepare_w("q", wq_sb)
-            slot(-3)
-            slot(-2)
+            scale_x(0)
+            quantize_x(0)
             prepare_w("k", wk_sb)
-            for i in range(-1, N_TILES + SCORE_LAG):
-                slot(i)
+            prepare_w("q", wq_sb)
+            for s in range(min(leads), n_pairs + max(leads)):
+                for stage, w, j, lead in order:
+                    p = s - lead
+                    if not 0 <= p < n_pairs:
+                        continue
+                    if p == 0 and stage in (widen, transpose_x, scale_x, quantize_x):
+                        continue
+                    if j is None:
+                        stage(p)
+                    elif w is None:
+                        stage(2 * p + j)
+                    else:
+                        stage(w, 2 * p + j)

@@ -29,7 +29,7 @@ def tile_llamaattention_pa_t_kernel(tc, x_bytes, x_scale, wq, wk, cos, sin, mask
         psum = ctx.enter_context(tc.psum_pool(name="psum", bufs=1))
 
         def bank(tag, bufs):
-            t = psum.tile([P, 512], F32, name=tag, tag=tag, bufs=bufs)
+            t = psum.tile([P, 512], F32, name=tag, tag="bank", bufs=8)
             return t
 
         scale_sb = keep.tile([P, 1, 4], F32, name="scale_sb")
@@ -52,11 +52,7 @@ def tile_llamaattention_pa_t_kernel(tc, x_bytes, x_scale, wq, wk, cos, sin, mask
         nc.scalar.dma_start(out=sin_sb[:], in_=sin.rearrange("(p j) d -> p j d", j=TILES))
         nc.scalar.dma_start(out=scale_sb[:], in_=x_scale.rearrange("a b (p t) -> p (a b) t", t=4))
         for w_dram, w_sb in ((wk, wk_sb), (wq, wq_sb)):
-            rows = w_dram.rearrange("(u g q t) k -> g u q t k", u=4, g=2, t=4)
-            for g in range(2):
-                for u in range(4):
-                    p0 = 64 * g + 16 * u
-                    nc.sync.dma_start(out=w_sb[p0 : p0 + 16], in_=rows[g, u])
+            nc.sync.dma_start(out=w_sb[:], in_=w_dram.rearrange("(p t) k -> p t k", t=4))
         load_x(0, 1024, 2048)
         load_x(1, 0, 2048)
         load_x(2, 0, 2048)
@@ -66,6 +62,11 @@ def tile_llamaattention_pa_t_kernel(tc, x_bytes, x_scale, wq, wk, cos, sin, mask
 
         ident = keep.tile([P, P], F32, name="ident")
         make_identity(nc, ident[:])
+        regroup = keep.tile([P, P], F32, name="regroup")
+        nc.vector.tensor_copy(
+            out=regroup[:].rearrange("p (g u q) -> p g u q", g=2, u=4),
+            in_=ident[:].rearrange("p (u g q) -> p g u q", u=4, g=2),
+        )
 
         cos_t = keep.tile([P, TILES, 4, 2, 4, 16], BF16, name="cos_t")
         sin_t = keep.tile([P, TILES, 4, 2, 4, 16], BF16, name="sin_t")
@@ -212,8 +213,8 @@ def tile_llamaattention_pa_t_kernel(tc, x_bytes, x_scale, wq, wk, cos, sin, mask
             )
 
         def quantize_rot(m):
-            rc = work.tile([P, 2, 256], U32, name="rot_codes", bufs=5, align_bytes=64)
-            rs = work.tile([P, 2, 256], U8, name="rot_scales", bufs=5, align_bytes=64)
+            rc = work.tile([P, 2, 256], U32, name="rot_codes", bufs=6, align_bytes=64)
+            rs = work.tile([P, 2, 256], U8, name="rot_scales", bufs=6, align_bytes=64)
             nc.vector.quantize_mx(
                 out=rc[:].rearrange("p w r -> p (w r)").bitcast(FP8X4),
                 scales=rs[:].rearrange("p w r -> p (w r)"),
@@ -268,7 +269,7 @@ def tile_llamaattention_pa_t_kernel(tc, x_bytes, x_scale, wq, wk, cos, sin, mask
                         nc.tensor.transpose(
                             wt[:, u * 256 + jt * P : u * 256 + (jt + 1) * P],
                             words[:, 256 * t + u : 256 * (t + 1) : 2],
-                            ident[:],
+                            regroup[:],
                         )
                 copy = nc.vector.tensor_copy if g == 0 else nc.scalar.copy
                 copy(
@@ -296,35 +297,35 @@ def tile_llamaattention_pa_t_kernel(tc, x_bytes, x_scale, wq, wk, cos, sin, mask
         n_pairs = N_TILES // 2
 
         order = [
-            (products_gpsimd, None, 0, -1),
-            (sum_and_turn, "k", 1, 0),
             (products_vector, "q", 0, -1),
-            (copy_k, None, 0, -2),
-            (sum_and_turn, "k", 0, -1),
+            (project, "k", 1, -2),
+            (products_gpsimd, None, 0, -2),
+            (transpose_x, None, None, -5),
+            (score, None, 0, 2),
+            (products_vector, "k", 0, 0),
             (products_vector, "q", 1, -1),
             (score, None, 1, 2),
-            (round_rot, "k", 1, 0),
-            (transpose_x, None, None, -5),
-            (finish, None, 1, 2),
-            (project, "k", 1, -2),
-            (sum_and_turn, "q", 0, -1),
             (round_rot, "k", 0, -1),
+            (sum_and_turn, "q", 0, -1),
+            (products_vector, "k", 1, -2),
+            (round_rot, "q", 1, 0),
+            (round_rot, "k", 1, 0),
+            (round_rot, "q", 0, -1),
+            (project, "k", 0, -3),
+            (scale_x, None, None, -5),
+            (copy_k, None, 1, -2),
+            (project, "q", 0, -2),
+            (finish, None, 0, 2),
+            (products_gpsimd, None, 1, -2),
             (quantize_x, None, None, -4),
             (quantize_rot, None, None, 0),
-            (sum_and_turn, "q", 1, -1),
-            (products_gpsimd, None, 1, -1),
-            (products_vector, "k", 1, -1),
-            (widen, None, None, -8),
-            (scale_x, None, None, -5),
-            (round_rot, "q", 0, -1),
-            (products_vector, "k", 0, -1),
-            (project, "q", 0, -2),
-            (copy_k, None, 1, -2),
-            (score, None, 0, 1),
-            (round_rot, "q", 1, -1),
-            (project, "k", 0, -3),
-            (finish, None, 0, 1),
+            (copy_k, None, 0, -3),
             (project, "q", 1, -2),
+            (widen, None, None, -7),
+            (sum_and_turn, "q", 1, -1),
+            (sum_and_turn, "k", 1, -1),
+            (sum_and_turn, "k", 0, -2),
+            (finish, None, 1, 2),
         ]
 
         leads = [lead for stage, w, j, lead in order]

@@ -81,6 +81,7 @@ def tile_llamaattention_pa_t_kernel(tc, x_bytes, x_scale, wq, wk, cos, sin, mask
 
         x_wide = {}
         x_t = {}
+        x_planes = {}
         x_grouped = {}
         x_codes = {}
         x_scales = {}
@@ -121,6 +122,25 @@ def tile_llamaattention_pa_t_kernel(tc, x_bytes, x_scale, wq, wk, cos, sin, mask
                 in1=scale_sb[:].to_broadcast([P, 256, 4]).rearrange("p r (u e) -> p r u e", e=2),
                 op=MULT,
             )
+            x_grouped[m] = xg
+
+        def scale_planes(m):
+            planes = work.tile([P, 4, 256], BF16, name="x_planes")
+            halves = x_t[m][:].bitcast(BF16).rearrange("p (u r e) -> p u e r", u=2, e=2)
+            for u in range(2):
+                for e in range(2):
+                    t = 2 * u + e
+                    nc.scalar.activation(
+                        out=planes[:, t, :],
+                        in_=halves[:, u, e, :],
+                        func=mybir.ActivationFunctionType.Copy,
+                        scale=scale_sb[:, 0, t : t + 1],
+                    )
+            x_planes[m] = planes
+
+        def interleave_planes(m):
+            xg = work.tile([P, 256, 4], BF16, name="x_grouped", bufs=4, align_bytes=64)
+            nc.scalar.copy(out=xg[:], in_=x_planes[m][:].rearrange("p t r -> p r t"))
             x_grouped[m] = xg
 
         def quantize_x(m):
@@ -242,7 +262,8 @@ def tile_llamaattention_pa_t_kernel(tc, x_bytes, x_scale, wq, wk, cos, sin, mask
 
         def finish(n):
             b, jj = divmod(n, TILES)
-            if jj % 2 == 0:
+            both = n // 2 in out_sb
+            if not both:
                 o = work.tile([P, 2, S], F32, name="out_sb")
                 out_sb[n // 2] = o
             o = out_sb[n // 2]
@@ -254,9 +275,9 @@ def tile_llamaattention_pa_t_kernel(tc, x_bytes, x_scale, wq, wk, cos, sin, mask
                 op0=MULT,
                 op1=ADD,
             )
-            if jj % 2 == 1:
+            if both:
                 rows = out[b].rearrange("(p j) n -> p j n", j=TILES)
-                nc.sync.dma_start(out=rows[:, jj - 1 : jj + 1, :], in_=o[:])
+                nc.sync.dma_start(out=rows[:, jj - jj % 2 : jj - jj % 2 + 2, :], in_=o[:])
 
         def prepare_w(w, w_sb):
             wg = keep.tile([P, H, 4], BF16, name="w_grouped_" + w, align_bytes=64)
@@ -297,38 +318,63 @@ def tile_llamaattention_pa_t_kernel(tc, x_bytes, x_scale, wq, wk, cos, sin, mask
         n_pairs = N_TILES // 2
 
         order = [
-            (products_vector, "q", 0, -1),
-            (project, "k", 1, -2),
-            (products_gpsimd, None, 0, -2),
-            (transpose_x, None, None, -5),
-            (score, None, 0, 2),
-            (products_vector, "k", 0, 0),
-            (products_vector, "q", 1, -1),
-            (score, None, 1, 2),
-            (round_rot, "k", 0, -1),
-            (sum_and_turn, "q", 0, -1),
-            (products_vector, "k", 1, -2),
-            (round_rot, "q", 1, 0),
-            (round_rot, "k", 1, 0),
-            (round_rot, "q", 0, -1),
-            (project, "k", 0, -3),
-            (scale_x, None, None, -5),
-            (copy_k, None, 1, -2),
-            (project, "q", 0, -2),
-            (finish, None, 0, 2),
-            (products_gpsimd, None, 1, -2),
-            (quantize_x, None, None, -4),
-            (quantize_rot, None, None, 0),
-            (copy_k, None, 0, -3),
-            (project, "q", 1, -2),
-            (widen, None, None, -7),
-            (sum_and_turn, "q", 1, -1),
-            (sum_and_turn, "k", 1, -1),
-            (sum_and_turn, "k", 0, -2),
-            (finish, None, 1, 2),
+            (products_vector, "q", 1, 1, 0),
+            (project, "q", 0, 1, 0),
+            (scale_x, None, None, 0, -2),
+            (sum_and_turn, "q", 1, 0, 0),
+            (products_gpsimd, None, 0, 0, 0),
+            (sum_and_turn, "k", 1, 0, 0),
+            (project, "k", 1, 1, 0),
+            (products_vector, "q", 0, 1, 0),
+            (round_rot, "k", 1, 1, 1),
+            (project, "q", 0, 0, -1),
+            (scale_planes, None, None, 1, -1),
+            (quantize_rot, None, None, 0, 1),
+            (sum_and_turn, "k", 0, 0, 0),
+            (interleave_planes, None, None, 1, -1),
+            (quantize_x, None, None, 0, -2),
+            (products_gpsimd, None, 0, 1, 0),
+            (sum_and_turn, "q", 1, 1, 0),
+            (round_rot, "q", 1, 0, 0),
+            (sum_and_turn, "k", 0, 1, 0),
+            (quantize_rot, None, None, 1, 1),
+            (quantize_x, None, None, 1, -1),
+            (score, None, 1, 1, 2),
+            (round_rot, "k", 1, 0, 0),
+            (score, None, 0, 0, 1),
+            (copy_k, None, 1, 1, 0),
+            (round_rot, "k", 0, 0, 0),
+            (round_rot, "q", 1, 1, 0),
+            (project, "k", 0, 0, -1),
+            (products_vector, "q", 0, 0, -1),
+            (score, None, 1, 0, 1),
+            (finish, None, 1, 1, 2),
+            (project, "k", 1, 0, -1),
+            (round_rot, "k", 0, 1, 0),
+            (finish, None, 0, 0, 1),
+            (score, None, 0, 1, 1),
+            (products_gpsimd, None, 1, 1, 0),
+            (copy_k, None, 0, 0, -1),
+            (widen, None, None, 1, -2),
+            (project, "k", 0, 1, -1),
+            (finish, None, 1, 0, 1),
+            (project, "q", 1, 0, -1),
+            (project, "q", 1, 1, -1),
+            (sum_and_turn, "q", 0, 1, 0),
+            (sum_and_turn, "q", 0, 0, -1),
+            (finish, None, 0, 1, 1),
+            (sum_and_turn, "k", 1, 1, 0),
+            (products_vector, "k", 1, 0, -1),
+            (widen, None, None, 0, -3),
+            (transpose_x, None, None, 1, -2),
+            (copy_k, None, 0, 1, -1),
+            (transpose_x, None, None, 0, -3),
+            (round_rot, "q", 0, 1, 0),
+            (products_vector, "q", 1, 0, -1),
+            (round_rot, "q", 0, 0, -1),
         ]
 
-        leads = [lead for stage, w, j, lead in order]
+        leads = [lead for stage, w, j, u, lead in order]
         with tc.manual_schedule():
             widen(0)
             transpose_x(0)
@@ -337,11 +383,12 @@ def tile_llamaattention_pa_t_kernel(tc, x_bytes, x_scale, wq, wk, cos, sin, mask
             quantize_x(0)
             prepare_w("k", wk_sb)
             prepare_w("q", wq_sb)
-            for s in range(min(leads), n_pairs + max(leads)):
-                for stage, w, j, lead in order:
-                    p = s - lead
-                    if not 0 <= p < n_pairs:
+            for s in range(min(leads), B + max(leads)):
+                for stage, w, j, u, lead in order:
+                    b = s - lead
+                    if not 0 <= b < B:
                         continue
+                    p = 2 * b + u
                     if p == 0 and stage in (widen, transpose_x, scale_x, quantize_x):
                         continue
                     if j is None:

from contextlib import ExitStack

import concourse.mybir as mybir
from concourse.masks import make_identity

F32 = mybir.dt.float32
BF16 = mybir.dt.bfloat16
U32 = mybir.dt.uint32
U8 = mybir.dt.uint8
FP8 = mybir.dt.float8_e4m3fn
FP8X4 = mybir.dt.float8_e4m3fn_x4
MULT = mybir.AluOpType.mult
ADD = mybir.AluOpType.add

B, S, H, HD = 8, 512, 512, 128
P = 128
TILES = S // P
N_TILES = B * TILES
FLOPS = 2 * B * S * H * H * 2 + 2 * B * S * S * H
SCORE_SCALE = 1.0 / HD**0.5
WHICH = {"q": 0, "k": 1}


def tile_llamaattention_pa_t_kernel(tc, x_bytes, x_scale, wq, wk, cos, sin, mask, out):
    nc = tc.nc
    with ExitStack() as ctx:
        keep = ctx.enter_context(tc.tile_pool(name="keep", bufs=1))
        work = ctx.enter_context(tc.tile_pool(name="work", bufs=3))
        psum = ctx.enter_context(tc.psum_pool(name="psum", bufs=1))

        def bank(tag, bufs):
            t = psum.tile([P, 512], F32, name=tag, tag="bank", bufs=8)
            return t

        scale_sb = keep.tile([P, 1, 4], F32, name="scale_sb")
        wq_sb = keep.tile([P, 4, H], BF16, name="wq_sb")
        wk_sb = keep.tile([P, 4, H], BF16, name="wk_sb")
        cos_sb = keep.tile([P, TILES, HD], BF16, name="cos_sb")
        sin_sb = keep.tile([P, TILES, HD], BF16, name="sin_sb")
        mask_sb = keep.tile([P, TILES, S], BF16, name="mask_sb")
        x_sb = []
        for b in range(B):
            xb = keep.tile([P, TILES * H], U8, name="x_bytes_sb%d" % b)
            x_sb.append(xb)

        def load_x(b, h0, h1):
            src = x_bytes[b].rearrange("(p j) k -> p (j k)", j=TILES)
            nc.sync.dma_start(out=x_sb[b][:, h0:h1], in_=src[:, h0:h1])

        load_x(0, 0, 1024)
        nc.scalar.dma_start(out=cos_sb[:], in_=cos.rearrange("(p j) d -> p j d", j=TILES))
        nc.scalar.dma_start(out=sin_sb[:], in_=sin.rearrange("(p j) d -> p j d", j=TILES))
        nc.scalar.dma_start(out=scale_sb[:], in_=x_scale.rearrange("a b (p t) -> p (a b) t", t=4))
        for w_dram, w_sb in ((wk, wk_sb), (wq, wq_sb)):
            nc.sync.dma_start(out=w_sb[:], in_=w_dram.rearrange("(p t) k -> p t k", t=4))
        load_x(0, 1024, 2048)
        load_x(1, 0, 2048)
        load_x(2, 0, 2048)
        nc.sync.dma_start(out=mask_sb[:], in_=mask.rearrange("a (p j) n -> p (a j) n", j=TILES))
        for b in range(3, B):
            load_x(b, 0, 2048)

        ident = keep.tile([P, P], F32, name="ident")
        make_identity(nc, ident[:])
        regroup = keep.tile([P, P], F32, name="regroup")
        nc.vector.tensor_copy(
            out=regroup[:].rearrange("p (g u q) -> p g u q", g=2, u=4),
            in_=ident[:].rearrange("p (u g q) -> p g u q", u=4, g=2),
        )

        cos_t = keep.tile([P, TILES, 4, 2, 4, 16], BF16, name="cos_t")
        sin_t = keep.tile([P, TILES, 4, 2, 4, 16], BF16, name="sin_t")

        w_codes = {}
        w_scales = {}
        for w in ("q", "k"):
            wc = keep.tile([P, H], U32, name="w_codes_" + w, align_bytes=64)
            ws = keep.tile([P, H], U8, name="w_scales_" + w, align_bytes=64)
            w_codes[w] = wc
            w_scales[w] = ws

        x_wide = {}
        x_t = {}
        x_planes = {}
        x_grouped = {}
        x_codes = {}
        x_scales = {}
        q_ps = {}
        k_ps = {}
        k_sb = {}
        prod = {}
        rot_ps = {}
        rot_grouped = {}
        rot_codes = {}
        rot_scales = {}
        score_ps = {}
        out_sb = {}

        def widen(m):
            xw = work.tile([P, 2 * H], BF16, name="x_wide", bufs=4)
            half = x_sb[m // 2][:, (m % 2) * 1024 : (m % 2) * 1024 + 1024]
            nc.scalar.copy(out=xw[:], in_=half.bitcast(FP8))
            x_wide[m] = xw

        def transpose_x(m):
            xt = bank("xt", 1)
            words = x_wide[m][:].bitcast(F32)
            for j in range(2):
                for u in range(2):
                    nc.tensor.transpose(
                        xt[:, u * 256 + j * P : u * 256 + (j + 1) * P],
                        words[:, 256 * j + u : 256 * (j + 1) : 2],
                        ident[:],
                    )
            x_t[m] = xt

        def scale_x(m):
            xg = work.tile([P, 256, 4], BF16, name="x_grouped", bufs=4, align_bytes=64)
            nc.vector.tensor_tensor(
                out=xg[:].rearrange("p r (u e) -> p r u e", e=2),
                in0=x_t[m][:].bitcast(BF16).rearrange("p (u r e) -> p r u e", u=2, e=2),
                in1=scale_sb[:].to_broadcast([P, 256, 4]).rearrange("p r (u e) -> p r u e", e=2),
                op=MULT,
            )
            x_grouped[m] = xg

        def scale_planes(m):
            planes = work.tile([P, 4, 256], BF16, name="x_planes")
            halves = x_t[m][:].bitcast(BF16).rearrange("p (u r e) -> p u e r", u=2, e=2)
            for u in range(2):
                for e in range(2):
                    t = 2 * u + e
                    nc.scalar.activation(
                        out=planes[:, t, :],
                        in_=halves[:, u, e, :],
                        func=mybir.ActivationFunctionType.Copy,
                        scale=scale_sb[:, 0, t : t + 1],
                    )
            x_planes[m] = planes

        def interleave_planes(m):
            xg = work.tile([P, 256, 4], BF16, name="x_grouped", bufs=4, align_bytes=64)
            nc.scalar.copy(out=xg[:], in_=x_planes[m][:].rearrange("p t r -> p r t"))
            x_grouped[m] = xg

        def quantize_x(m):
            xc = work.tile([P, 256], U32, name="x_codes", bufs=6, align_bytes=64)
            xs = work.tile([P, 256], U8, name="x_scales", bufs=6, align_bytes=64)
            nc.vector.quantize_mx(
                out=xc[:].bitcast(FP8X4), scales=xs[:], in_=x_grouped[m][:].rearrange("p r t -> p (r t)")
            )
            x_codes[m] = xc
            x_scales[m] = xs

        def project(w, i):
            m, j = divmod(i, 2)
            cols = slice(j * P, (j + 1) * P)
            if w == "q":
                acc = bank("q_ps", 2)
                q_ps[i] = acc
            elif on_gpsimd(i):
                acc = bank("kg_ps", 1)
                k_ps[i] = acc
            else:
                acc = bank("kv_ps", 1)
                k_ps[i] = acc
            nc.tensor.matmul_mx(
                out=acc[:],
                lhsT=x_codes[m][:, cols].bitcast(FP8X4),
                lhsT_scale=x_scales[m][:, cols],
                rhs=w_codes[w][:].bitcast(FP8X4),
                rhs_scale=w_scales[w][:],
                start=True,
                stop=True,
            )

        def on_gpsimd(i):
            return i % 4 != 1

        def copy_k(i):
            if not on_gpsimd(i):
                return
            kf = work.tile([P, H], F32, name="k_sb", bufs=2)
            nc.scalar.copy(out=kf[:], in_=k_ps[i][:])
            k_sb[i] = kf

        def rope_products(engine, w, i, src):
            jj = i % TILES
            direct = work.tile([P, H], F32, name="direct_" + w + ("g" if engine is nc.gpsimd else "v"), bufs=2)
            engine.tensor_tensor(
                out=direct[:], in0=src[:], in1=cos_t[:, jj].rearrange("p t g u q -> p (t g u q)"), op=MULT
            )
            crossed = work.tile([P, H], F32, name="crossed_" + w + ("g" if engine is nc.gpsimd else "v"), bufs=2)
            engine.tensor_tensor(
                out=crossed[:].rearrange("p (t g c) -> p t g c", t=4, g=2),
                in0=src[:].rearrange("p (t g c) -> p t g c", t=4, g=2)[:, :, ::-1, :],
                in1=sin_t[:, jj].rearrange("p t g u q -> p t g (u q)"),
                op=MULT,
            )
            prod[w, i] = (direct, crossed)

        def products_gpsimd(i):
            if on_gpsimd(i):
                rope_products(nc.gpsimd, "k", i, k_sb[i])

        def products_vector(w, i):
            if w == "q":
                rope_products(nc.vector, "q", i, q_ps[i])
            elif not on_gpsimd(i):
                rope_products(nc.vector, "k", i, k_ps[i])

        def sum_and_turn(w, i):
            rot = bank("rot", 2)
            direct, crossed = prod[w, i]
            for t in range(4):
                cols = slice(t * P, (t + 1) * P)
                nc.tensor.matmul(
                    rot[:, cols], lhsT=direct[:, cols], rhs=ident[:], start=True, stop=False, is_transpose=True
                )
                nc.tensor.matmul(
                    rot[:, cols], lhsT=crossed[:, cols], rhs=ident[:], start=False, stop=True, is_transpose=True
                )
            rot_ps[w, i] = rot

        def round_rot(w, i):
            m, j = divmod(i, 2)
            if m not in rot_grouped:
                rg = work.tile([P, 2, 256, 4], BF16, name="rot_grouped", bufs=3, align_bytes=64)
                rot_grouped[m] = rg
            nc.scalar.copy(
                out=rot_grouped[m][:, WHICH[w], j * P : (j + 1) * P, :],
                in_=rot_ps[w, i][:].rearrange("p (t r) -> p r t", t=4),
            )

        def quantize_rot(m):
            rc = work.tile([P, 2, 256], U32, name="rot_codes", bufs=6, align_bytes=64)
            rs = work.tile([P, 2, 256], U8, name="rot_scales", bufs=6, align_bytes=64)
            nc.vector.quantize_mx(
                out=rc[:].rearrange("p w r -> p (w r)").bitcast(FP8X4),
                scales=rs[:].rearrange("p w r -> p (w r)"),
                in_=rot_grouped[m][:].rearrange("p w r t -> p (w r t)"),
            )
            rot_codes[m] = rc
            rot_scales[m] = rs

        def score(n):
            m, j = divmod(n, 2)
            cols = slice(j * P, (j + 1) * P)
            first = m - m % 2
            acc = bank("score", 1)
            for h in range(2):
                nc.tensor.matmul_mx(
                    out=acc[:, h * 256 : (h + 1) * 256],
                    lhsT=rot_codes[m][:, 0, cols].bitcast(FP8X4),
                    lhsT_scale=rot_scales[m][:, 0, cols],
                    rhs=rot_codes[first + h][:, 1, :].bitcast(FP8X4),
                    rhs_scale=rot_scales[first + h][:, 1, :],
                    start=True,
                    stop=True,
                )
            score_ps[n] = acc

        def finish(n):
            b, jj = divmod(n, TILES)
            both = n // 2 in out_sb
            if not both:
                o = work.tile([P, 2, S], F32, name="out_sb")
                out_sb[n // 2] = o
            o = out_sb[n // 2]
            nc.vector.scalar_tensor_tensor(
                out=o[:, jj % 2, :].rearrange("p (r j) -> p r j", j=TILES),
                in0=score_ps[n][:].rearrange("p (j r) -> p r j", j=TILES),
                scalar=SCORE_SCALE,
                in1=mask_sb[:, jj, :].rearrange("p (r j) -> p r j", j=TILES),
                op0=MULT,
                op1=ADD,
            )
            if both:
                rows = out[b].rearrange("(p j) n -> p j n", j=TILES)
                nc.sync.dma_start(out=rows[:, jj - jj % 2 : jj - jj % 2 + 2, :], in_=o[:])

        def prepare_w(w, w_sb):
            wg = keep.tile([P, H, 4], BF16, name="w_grouped_" + w, align_bytes=64)
            words = w_sb[:].rearrange("p t k -> p (t k)").bitcast(F32)
            for g in range(2):
                wt = bank("rot", 2)
                for jt in range(2):
                    t = 2 * g + jt
                    for u in range(2):
                        nc.tensor.transpose(
                            wt[:, u * 256 + jt * P : u * 256 + (jt + 1) * P],
                            words[:, 256 * t + u : 256 * (t + 1) : 2],
                            regroup[:],
                        )
                copy = nc.vector.tensor_copy if g == 0 else nc.scalar.copy
                copy(
                    out=wg[:, g * 256 : (g + 1) * 256, :].rearrange("p f t -> p (f t)").bitcast(F32),
                    in_=wt[:].rearrange("p (u f) -> p f u", u=2),
                )
            nc.vector.quantize_mx(
                out=w_codes[w][:].bitcast(FP8X4), scales=w_scales[w][:], in_=wg[:].rearrange("p f t -> p (f t)")
            )

        def build_tables():
            for g in range(2):
                for u in range(4):
                    nc.vector.tensor_copy(
                        out=cos_t[:, :, :, g, u, :],
                        in_=cos_sb[:].rearrange("p j (g q t) -> p j t g q", g=2, t=4)[:, :, :, g, :],
                    )
                    nc.scalar.activation(
                        out=sin_t[:, :, :, g, u, :],
                        in_=sin_sb[:].rearrange("p j (g q t) -> p j t g q", g=2, t=4)[:, :, :, g, :],
                        func=mybir.ActivationFunctionType.Copy,
                        scale=-1.0 if g == 0 else 1.0,
                    )

        n_pairs = N_TILES // 2

        order = [
            (products_vector, "q", 1, 1, 0),
            (project, "q", 0, 1, 0),
            (scale_x, None, None, 0, -2),
            (sum_and_turn, "q", 1, 0, 0),
            (products_gpsimd, None, 0, 0, 0),
            (sum_and_turn, "k", 1, 0, 0),
            (project, "k", 1, 1, 0),
            (products_vector, "q", 0, 1, 0),
            (round_rot, "k", 1, 1, 1),
            (project, "q", 0, 0, -1),
            (scale_planes, None, None, 1, -1),
            (quantize_rot, None, None, 0, 1),
            (sum_and_turn, "k", 0, 0, 0),
            (interleave_planes, None, None, 1, -1),
            (quantize_x, None, None, 0, -2),
            (products_gpsimd, None, 0, 1, 0),
            (sum_and_turn, "q", 1, 1, 0),
            (round_rot, "q", 1, 0, 0),
            (sum_and_turn, "k", 0, 1, 0),
            (quantize_rot, None, None, 1, 1),
            (quantize_x, None, None, 1, -1),
            (score, None, 1, 1, 2),
            (round_rot, "k", 1, 0, 0),
            (score, None, 0, 0, 1),
            (copy_k, None, 1, 1, 0),
            (round_rot, "k", 0, 0, 0),
            (round_rot, "q", 1, 1, 0),
            (project, "k", 0, 0, -1),
            (products_vector, "q", 0, 0, -1),
            (score, None, 1, 0, 1),
            (finish, None, 1, 1, 2),
            (project, "k", 1, 0, -1),
            (round_rot, "k", 0, 1, 0),
            (finish, None, 0, 0, 1),
            (score, None, 0, 1, 1),
            (products_gpsimd, None, 1, 1, 0),
            (copy_k, None, 0, 0, -1),
            (widen, None, None, 1, -2),
            (project, "k", 0, 1, -1),
            (finish, None, 1, 0, 1),
            (project, "q", 1, 0, -1),
            (project, "q", 1, 1, -1),
            (sum_and_turn, "q", 0, 1, 0),
            (sum_and_turn, "q", 0, 0, -1),
            (finish, None, 0, 1, 1),
            (sum_and_turn, "k", 1, 1, 0),
            (products_vector, "k", 1, 0, -1),
            (widen, None, None, 0, -3),
            (transpose_x, None, None, 1, -2),
            (copy_k, None, 0, 1, -1),
            (transpose_x, None, None, 0, -3),
            (round_rot, "q", 0, 1, 0),
            (products_vector, "q", 1, 0, -1),
            (round_rot, "q", 0, 0, -1),
        ]

        leads = [lead for stage, w, j, u, lead in order]
        with tc.manual_schedule():
            widen(0)
            transpose_x(0)
            build_tables()
            scale_x(0)
            quantize_x(0)
            prepare_w("k", wk_sb)
            prepare_w("q", wq_sb)
            for s in range(min(leads), B + max(leads)):
                for stage, w, j, u, lead in order:
                    b = s - lead
                    if not 0 <= b < B:
                        continue
                    p = 2 * b + u
                    if p == 0 and stage in (widen, transpose_x, scale_x, quantize_x):
                        continue
                    if j is None:
                        stage(p)
                    elif w is None:
                        stage(2 * p + j)
                    else:
                        stage(w, 2 * p + j)
